import numpy as np
import ml_dtypes

BF16 = ml_dtypes.bfloat16


def bf(x):
    return np.asarray(x, np.float32).astype(BF16)


def f32(x):
    return np.asarray(x, np.float32)


def f64(x):
    return np.asarray(x).astype(np.float64)


def striped(idx):
    return np.tile(idx.reshape(-1, 16).T, (8, 1))


P, S, N, B, C = 128, 1024, 512, 4, 128
SLOPE = 0.01
FSCALE = 0.25
SHIFT = 0.5


def leaky(v):
    return np.maximum(v, SLOPE * v)


def setup_inputs():
    return {"rf": f32(np.random.standard_normal((P, S)) - SHIFT), "fmap": bf(FSCALE * np.random.standard_normal((P, B * C))), "w": f32(np.random.standard_normal((C, N))), "offs": striped(np.random.permutation(S)[:N])}


def reference(rf, fmap, w, offs):
    idx = offs[:16].T.reshape(-1)
    a = leaky(f64(rf)[:, idx])
    proj = f64(fmap).T @ a
    return (proj.reshape(B, C, N) * f64(w)[None, :, :]).reshape(B * C, N)

@@ -1,0 +1,48 @@
+import concourse.mybir as mybir
+
+PIXELS = 128
+VOXELS = 1024
+PICKED = 512
+IMAGES = 4
+CHANNELS = 128
+SLOPE = 0.01
+
+FLOPS = 2 * PIXELS * IMAGES * CHANNELS * PICKED
+
+F32 = mybir.dt.float32
+BF16 = mybir.dt.bfloat16
+U16 = mybir.dt.uint16
+COPY = mybir.ActivationFunctionType.Copy
+MULT = mybir.AluOpType.mult
+MAX = mybir.AluOpType.max
+
+
+def tile_simple_model_terms_kernel(tc, rf, fmap, w, offs, out):
+    nc = tc.nc
+    with (
+        tc.tile_pool(name="held", bufs=1) as held,
+        tc.tile_pool(name="results", bufs=IMAGES) as results,
+        tc.psum_pool(name="banks", bufs=IMAGES) as banks,
+    ):
+        offsets = held.tile([PIXELS, PICKED // 16], U16, name="offsets")
+        nc.sync.dma_start(offsets[:], offs)
+        fields = held.tile([PIXELS, VOXELS], F32, name="fields")
+        nc.sync.dma_start(fields[:], rf)
+        maps = held.tile([PIXELS, IMAGES * CHANNELS], BF16, name="maps")
+        nc.scalar.dma_start(maps[:], fmap)
+        weights = held.tile([CHANNELS, PICKED], F32, name="weights")
+        nc.scalar.dma_start(weights[:], w)
+
+        picked = held.tile([PIXELS, PICKED], F32, name="picked")
+        nc.scalar.activation(picked[:], fields[:].indirect(offsets[:]), COPY)
+
+        rectified = held.tile([PIXELS, PICKED], BF16, name="rectified")
+        nc.vector.scalar_tensor_tensor(rectified[:], picked[:], SLOPE, picked[:], MULT, MAX)
+
+        for b in range(IMAGES):
+            rows = slice(b * CHANNELS, (b + 1) * CHANNELS)
+            pooled = banks.tile([CHANNELS, PICKED], F32, name="pooled")
+            nc.tensor.matmul(pooled[:], maps[:, rows], rectified[:], start=True, stop=True)
+            scaled = results.tile([CHANNELS, PICKED], F32, name="scaled")
+            nc.vector.tensor_tensor(scaled[:], pooled[:], weights[:], MULT)
+            nc.sync.dma_start(out[rows, :], scaled[:])

@@ -33,6 +33,11 @@ def tile_simple_model_terms_kernel(tc, rf, fmap, w, offs, out):
         weights = held.tile([CHANNELS, PICKED], F32, name="weights")
         nc.scalar.dma_start(weights[:], w)
 
+        scratch = held.tile([PIXELS, 1], F32, name="scratch")
+        nc.vector.memset(scratch[:], 0.0)
+        warmed = held.tile([PIXELS, 1], F32, name="warmed")
+        nc.scalar.activation(warmed[:], scratch[:], COPY)
+
         picked = held.tile([PIXELS, PICKED], F32, name="picked")
         nc.scalar.activation(picked[:], fields[:].indirect(offsets[:]), COPY)
 

@@ -27,9 +27,12 @@ def tile_simple_model_terms_kernel(tc, rf, fmap, w, offs, out):
         offsets = held.tile([PIXELS, PICKED // 16], U16, name="offsets")
         nc.sync.dma_start(offsets[:], offs)
         fields = held.tile([PIXELS, VOXELS], F32, name="fields")
-        nc.sync.dma_start(fields[:], rf)
+        quarter = VOXELS // 4
+        for q, queue in enumerate((nc.sync, nc.scalar, nc.sync, nc.scalar)):
+            columns = slice(q * quarter, (q + 1) * quarter)
+            queue.dma_start(fields[:, columns], rf[:, columns])
         maps = held.tile([PIXELS, IMAGES * CHANNELS], BF16, name="maps")
-        nc.scalar.dma_start(maps[:], fmap)
+        nc.sync.dma_start(maps[:], fmap)
         weights = held.tile([CHANNELS, PICKED], F32, name="weights")
         nc.scalar.dma_start(weights[:], w)
 

@@ -6,6 +6,8 @@ PICKED = 512
 IMAGES = 4
 CHANNELS = 128
 SLOPE = 0.01
+PIECES = 2
+PIECE = PICKED // PIECES
 
 FLOPS = 2 * PIXELS * IMAGES * CHANNELS * PICKED
 
@@ -21,8 +23,9 @@ def tile_simple_model_terms_kernel(tc, rf, fmap, w, offs, out):
     nc = tc.nc
     with (
         tc.tile_pool(name="held", bufs=1) as held,
-        tc.tile_pool(name="results", bufs=IMAGES) as results,
-        tc.psum_pool(name="banks", bufs=IMAGES) as banks,
+        tc.tile_pool(name="halves", bufs=PIECES) as halves,
+        tc.tile_pool(name="results", bufs=PIECES * IMAGES) as results,
+        tc.psum_pool(name="banks", bufs=PIECES * IMAGES) as banks,
     ):
         offsets = held.tile([PIXELS, PICKED // 16], U16, name="offsets")
         nc.sync.dma_start(offsets[:], offs)
@@ -41,16 +44,19 @@ def tile_simple_model_terms_kernel(tc, rf, fmap, w, offs, out):
         warmed = held.tile([PIXELS, 1], F32, name="warmed")
         nc.scalar.activation(warmed[:], scratch[:], COPY)
 
-        picked = held.tile([PIXELS, PICKED], F32, name="picked")
-        nc.scalar.activation(picked[:], fields[:].indirect(offsets[:]), COPY)
+        for k in range(PIECES):
+            columns = slice(k * PIECE, (k + 1) * PIECE)
+            picked = halves.tile([PIXELS, PIECE], F32, name="picked")
+            listed = offsets[:, k * PIECE // 16 : (k + 1) * PIECE // 16]
+            nc.scalar.activation(picked[:], fields[:].indirect(listed), COPY)
 
-        rectified = held.tile([PIXELS, PICKED], BF16, name="rectified")
-        nc.vector.scalar_tensor_tensor(rectified[:], picked[:], SLOPE, picked[:], MULT, MAX)
+            rectified = halves.tile([PIXELS, PIECE], BF16, name="rectified")
+            nc.vector.scalar_tensor_tensor(rectified[:], picked[:], SLOPE, picked[:], MULT, MAX)
 
-        for b in range(IMAGES):
-            rows = slice(b * CHANNELS, (b + 1) * CHANNELS)
-            pooled = banks.tile([CHANNELS, PICKED], F32, name="pooled")
-            nc.tensor.matmul(pooled[:], maps[:, rows], rectified[:], start=True, stop=True)
-            scaled = results.tile([CHANNELS, PICKED], F32, name="scaled")
-            nc.vector.tensor_tensor(scaled[:], pooled[:], weights[:], MULT)
-            nc.sync.dma_start(out[rows, :], scaled[:])
+            for b in range(IMAGES):
+                rows = slice(b * CHANNELS, (b + 1) * CHANNELS)
+                pooled = banks.tile([CHANNELS, PIECE], F32, name="pooled")
+                nc.tensor.matmul(pooled[:], maps[:, rows], rectified[:], start=True, stop=True)
+                scaled = results.tile([CHANNELS, PIECE], F32, name="scaled")
+                nc.vector.tensor_tensor(scaled[:], pooled[:], weights[:, columns], MULT)
+                nc.sync.dma_start(out[rows, columns], scaled[:])

@@ -6,8 +6,10 @@ PICKED = 512
 IMAGES = 4
 CHANNELS = 128
 SLOPE = 0.01
-PIECES = 2
-PIECE = PICKED // PIECES
+WIDTHS = (64, 128, 256, 64)
+assert sum(WIDTHS) == PICKED
+BLOCK = 256
+BLOCKS = IMAGES * PICKED // BLOCK
 
 FLOPS = 2 * PIXELS * IMAGES * CHANNELS * PICKED
 
@@ -23,9 +25,9 @@ def tile_simple_model_terms_kernel(tc, rf, fmap, w, offs, out):
     nc = tc.nc
     with (
         tc.tile_pool(name="held", bufs=1) as held,
-        tc.tile_pool(name="halves", bufs=PIECES) as halves,
-        tc.tile_pool(name="results", bufs=PIECES * IMAGES) as results,
-        tc.psum_pool(name="banks", bufs=PIECES * IMAGES) as banks,
+        tc.tile_pool(name="pieces", bufs=len(WIDTHS)) as pieces,
+        tc.tile_pool(name="results", bufs=BLOCKS) as results,
+        tc.psum_pool(name="banks", bufs=BLOCKS) as banks,
     ):
         offsets = held.tile([PIXELS, PICKED // 16], U16, name="offsets")
         nc.sync.dma_start(offsets[:], offs)
@@ -44,19 +46,34 @@ def tile_simple_model_terms_kernel(tc, rf, fmap, w, offs, out):
         warmed = held.tile([PIXELS, 1], F32, name="warmed")
         nc.scalar.activation(warmed[:], scratch[:], COPY)
 
-        for k in range(PIECES):
-            columns = slice(k * PIECE, (k + 1) * PIECE)
-            picked = halves.tile([PIXELS, PIECE], F32, name="picked")
-            listed = offsets[:, k * PIECE // 16 : (k + 1) * PIECE // 16]
+        starts = [sum(WIDTHS[:k]) for k in range(len(WIDTHS))]
+
+        def look_up(k):
+            start, width = starts[k], WIDTHS[k]
+            picked = pieces.tile([PIXELS, width], F32, name="picked")
+            listed = offsets[:, start // 16 : (start + width) // 16]
             nc.scalar.activation(picked[:], fields[:].indirect(listed), COPY)
-
-            rectified = halves.tile([PIXELS, PIECE], BF16, name="rectified")
+            rectified = pieces.tile([PIXELS, width], BF16, name="rectified")
             nc.vector.scalar_tensor_tensor(rectified[:], picked[:], SLOPE, picked[:], MULT, MAX)
+            return rectified
 
-            for b in range(IMAGES):
-                rows = slice(b * CHANNELS, (b + 1) * CHANNELS)
-                pooled = banks.tile([CHANNELS, PIECE], F32, name="pooled")
-                nc.tensor.matmul(pooled[:], maps[:, rows], rectified[:], start=True, stop=True)
-                scaled = results.tile([CHANNELS, PIECE], F32, name="scaled")
-                nc.vector.tensor_tensor(scaled[:], pooled[:], weights[:, columns], MULT)
-                nc.sync.dma_start(out[rows, columns], scaled[:])
+        def pool_and_scale(k, rectified):
+            width = WIDTHS[k]
+            columns = slice(starts[k], starts[k] + width)
+            sharing = BLOCK // width
+            repeated = weights[:, columns].unsqueeze(1).to_broadcast([CHANNELS, sharing, width])
+            for first in range(0, IMAGES, sharing):
+                pooled = banks.tile([CHANNELS, sharing, width], F32, name="pooled")
+                for i in range(sharing):
+                    rows = slice((first + i) * CHANNELS, (first + i + 1) * CHANNELS)
+                    nc.tensor.matmul(pooled[:, i, :], maps[:, rows], rectified[:], start=True, stop=True)
+                scaled = results.tile([CHANNELS, sharing, width], F32, name="scaled")
+                nc.vector.tensor_tensor(scaled[:], pooled[:], repeated, MULT)
+                block = out[first * CHANNELS : (first + sharing) * CHANNELS, columns]
+                nc.sync.dma_start(block.rearrange("(i c) j -> c i j", c=CHANNELS), scaled[:])
+
+        ready = look_up(0)
+        for k in range(len(WIDTHS)):
+            ahead = look_up(k + 1) if k + 1 < len(WIDTHS) else None
+            pool_and_scale(k, ready)
+            ready = ahead

@@ -6,7 +6,7 @@ PICKED = 512
 IMAGES = 4
 CHANNELS = 128
 SLOPE = 0.01
-WIDTHS = (64, 128, 256, 64)
+WIDTHS = (128, 128, 128, 128)
 assert sum(WIDTHS) == PICKED
 BLOCK = 256
 BLOCKS = IMAGES * PICKED // BLOCK

@@ -6,10 +6,11 @@ PICKED = 512
 IMAGES = 4
 CHANNELS = 128
 SLOPE = 0.01
-WIDTHS = (128, 128, 128, 128)
+WIDTHS = (128, 128, 256)
 assert sum(WIDTHS) == PICKED
 BLOCK = 256
-BLOCKS = IMAGES * PICKED // BLOCK
+BLOCKS = IMAGES * PICKED // BLOCK + 1
+BANKS = 8
 
 FLOPS = 2 * PIXELS * IMAGES * CHANNELS * PICKED
 
@@ -27,15 +28,15 @@ def tile_simple_model_terms_kernel(tc, rf, fmap, w, offs, out):
         tc.tile_pool(name="held", bufs=1) as held,
         tc.tile_pool(name="pieces", bufs=len(WIDTHS)) as pieces,
         tc.tile_pool(name="results", bufs=BLOCKS) as results,
-        tc.psum_pool(name="banks", bufs=BLOCKS) as banks,
+        tc.psum_pool(name="banks", bufs=BANKS) as banks,
     ):
-        offsets = held.tile([PIXELS, PICKED // 16], U16, name="offsets")
-        nc.sync.dma_start(offsets[:], offs)
         fields = held.tile([PIXELS, VOXELS], F32, name="fields")
         quarter = VOXELS // 4
         for q, queue in enumerate((nc.sync, nc.scalar, nc.sync, nc.scalar)):
             columns = slice(q * quarter, (q + 1) * quarter)
             queue.dma_start(fields[:, columns], rf[:, columns])
+        offsets = held.tile([PIXELS, PICKED // 16], U16, name="offsets")
+        nc.sync.dma_start(offsets[:], offs)
         maps = held.tile([PIXELS, IMAGES * CHANNELS], BF16, name="maps")
         nc.sync.dma_start(maps[:], fmap)
         weights = held.tile([CHANNELS, PICKED], F32, name="weights")
@@ -60,9 +61,12 @@ def tile_simple_model_terms_kernel(tc, rf, fmap, w, offs, out):
         def pool_and_scale(k, rectified):
             width = WIDTHS[k]
             columns = slice(starts[k], starts[k] + width)
-            sharing = BLOCK // width
-            repeated = weights[:, columns].unsqueeze(1).to_broadcast([CHANNELS, sharing, width])
-            for first in range(0, IMAGES, sharing):
+            sharings = [BLOCK // width] * (IMAGES * width // BLOCK)
+            if k == 0:
+                sharings = [1] * sharings[0] + sharings[1:]
+            for n, sharing in enumerate(sharings):
+                first = sum(sharings[:n])
+                repeated = weights[:, columns].unsqueeze(1).to_broadcast([CHANNELS, sharing, width])
                 pooled = banks.tile([CHANNELS, sharing, width], F32, name="pooled")
                 for i in range(sharing):
                     rows = slice((first + i) * CHANNELS, (first + i + 1) * CHANNELS)

@@ -31,9 +31,9 @@ def tile_simple_model_terms_kernel(tc, rf, fmap, w, offs, out):
         tc.psum_pool(name="banks", bufs=BANKS) as banks,
     ):
         fields = held.tile([PIXELS, VOXELS], F32, name="fields")
-        quarter = VOXELS // 4
-        for q, queue in enumerate((nc.sync, nc.scalar, nc.sync, nc.scalar)):
-            columns = slice(q * quarter, (q + 1) * quarter)
+        half = VOXELS // 2
+        for h, queue in enumerate((nc.sync, nc.scalar)):
+            columns = slice(h * half, (h + 1) * half)
             queue.dma_start(fields[:, columns], rf[:, columns])
         offsets = held.tile([PIXELS, PICKED // 16], U16, name="offsets")
         nc.sync.dma_start(offsets[:], offs)

@@ -6,7 +6,7 @@ PICKED = 512
 IMAGES = 4
 CHANNELS = 128
 SLOPE = 0.01
-WIDTHS = (128, 128, 256)
+WIDTHS = (128, 128, 128, 128)
 assert sum(WIDTHS) == PICKED
 BLOCK = 256
 BLOCKS = IMAGES * PICKED // BLOCK + 1

@@ -39,8 +39,9 @@ def tile_simple_model_terms_kernel(tc, rf, fmap, w, offs, out):
         nc.sync.dma_start(offsets[:], offs)
         maps = held.tile([PIXELS, IMAGES * CHANNELS], BF16, name="maps")
         nc.sync.dma_start(maps[:], fmap)
-        weights = held.tile([CHANNELS, PICKED], F32, name="weights")
-        nc.scalar.dma_start(weights[:], w)
+        weights = [held.tile([CHANNELS, PICKED // 2], F32, name=f"weights{h}") for h in range(2)]
+        for h in range(2):
+            nc.sync.dma_start(weights[h][:], w[:, h * PICKED // 2 : (h + 1) * PICKED // 2])
 
         scratch = held.tile([PIXELS, 1], F32, name="scratch")
         nc.vector.memset(scratch[:], 0.0)
@@ -66,7 +67,9 @@ def tile_simple_model_terms_kernel(tc, rf, fmap, w, offs, out):
                 sharings = [1] * sharings[0] + sharings[1:]
             for n, sharing in enumerate(sharings):
                 first = sum(sharings[:n])
-                repeated = weights[:, columns].unsqueeze(1).to_broadcast([CHANNELS, sharing, width])
+                share = weights[starts[k] * 2 // PICKED]
+                local = slice(starts[k] % (PICKED // 2), starts[k] % (PICKED // 2) + width)
+                repeated = share[:, local].unsqueeze(1).to_broadcast([CHANNELS, sharing, width])
                 pooled = banks.tile([CHANNELS, sharing, width], F32, name="pooled")
                 for i in range(sharing):
                     rows = slice((first + i) * CHANNELS, (first + i + 1) * CHANNELS)

@@ -31,10 +31,7 @@ def tile_simple_model_terms_kernel(tc, rf, fmap, w, offs, out):
         tc.psum_pool(name="banks", bufs=BANKS) as banks,
     ):
         fields = held.tile([PIXELS, VOXELS], F32, name="fields")
-        half = VOXELS // 2
-        for h, queue in enumerate((nc.sync, nc.scalar)):
-            columns = slice(h * half, (h + 1) * half)
-            queue.dma_start(fields[:, columns], rf[:, columns])
+        nc.sync.dma_start(fields[:], rf)
         offsets = held.tile([PIXELS, PICKED // 16], U16, name="offsets")
         nc.sync.dma_start(offsets[:], offs)
         maps = held.tile([PIXELS, IMAGES * CHANNELS], BF16, name="maps")

@@ -18,7 +18,9 @@ F32 = mybir.dt.float32
 BF16 = mybir.dt.bfloat16
 U16 = mybir.dt.uint16
 COPY = mybir.ActivationFunctionType.Copy
+RELU = mybir.ActivationFunctionType.Relu
 MULT = mybir.AluOpType.mult
+SUBTRACT = mybir.AluOpType.subtract
 MAX = mybir.AluOpType.max
 
 
@@ -53,7 +55,14 @@ def tile_simple_model_terms_kernel(tc, rf, fmap, w, offs, out):
             listed = offsets[:, start // 16 : (start + width) // 16]
             nc.scalar.activation(picked[:], fields[:].indirect(listed), COPY)
             rectified = pieces.tile([PIXELS, width], BF16, name="rectified")
-            nc.vector.scalar_tensor_tensor(rectified[:], picked[:], SLOPE, picked[:], MULT, MAX)
+            if k < len(WIDTHS) - 1:
+                nc.vector.scalar_tensor_tensor(rectified[:], picked[:], SLOPE, picked[:], MULT, MAX)
+            else:
+                above = pieces.tile([PIXELS, width], F32, name="above")
+                nc.scalar.activation(above[:], picked[:], RELU)
+                below = pieces.tile([PIXELS, width], F32, name="below")
+                nc.scalar.activation(below[:], picked[:], RELU, scale=-SLOPE)
+                nc.gpsimd.tensor_tensor(rectified[:], above[:], below[:], SUBTRACT)
             return rectified
 
         def pool_and_scale(k, rectified):

@@ -20,7 +20,7 @@ U16 = mybir.dt.uint16
 COPY = mybir.ActivationFunctionType.Copy
 RELU = mybir.ActivationFunctionType.Relu
 MULT = mybir.AluOpType.mult
-SUBTRACT = mybir.AluOpType.subtract
+ADD = mybir.AluOpType.add
 MAX = mybir.AluOpType.max
 
 
@@ -58,11 +58,9 @@ def tile_simple_model_terms_kernel(tc, rf, fmap, w, offs, out):
             if k < len(WIDTHS) - 1:
                 nc.vector.scalar_tensor_tensor(rectified[:], picked[:], SLOPE, picked[:], MULT, MAX)
             else:
-                above = pieces.tile([PIXELS, width], F32, name="above")
-                nc.scalar.activation(above[:], picked[:], RELU)
-                below = pieces.tile([PIXELS, width], F32, name="below")
-                nc.scalar.activation(below[:], picked[:], RELU, scale=-SLOPE)
-                nc.gpsimd.tensor_tensor(rectified[:], above[:], below[:], SUBTRACT)
+                lift = pieces.tile([PIXELS, width], F32, name="lift")
+                nc.scalar.activation(lift[:], picked[:], RELU, scale=SLOPE - 1.0)
+                nc.gpsimd.tensor_tensor(rectified[:], picked[:], lift[:], ADD)
             return rectified
 
         def pool_and_scale(k, rectified):

import concourse.mybir as mybir

PIXELS = 128
VOXELS = 1024
PICKED = 512
IMAGES = 4
CHANNELS = 128
SLOPE = 0.01
WIDTHS = (128, 128, 128, 128)
assert sum(WIDTHS) == PICKED
BLOCK = 256
BLOCKS = IMAGES * PICKED // BLOCK + 1
BANKS = 8

FLOPS = 2 * PIXELS * IMAGES * CHANNELS * PICKED

F32 = mybir.dt.float32
BF16 = mybir.dt.bfloat16
U16 = mybir.dt.uint16
COPY = mybir.ActivationFunctionType.Copy
RELU = mybir.ActivationFunctionType.Relu
MULT = mybir.AluOpType.mult
ADD = mybir.AluOpType.add
MAX = mybir.AluOpType.max


def tile_simple_model_terms_kernel(tc, rf, fmap, w, offs, out):
    nc = tc.nc
    with (
        tc.tile_pool(name="held", bufs=1) as held,
        tc.tile_pool(name="pieces", bufs=len(WIDTHS)) as pieces,
        tc.tile_pool(name="results", bufs=BLOCKS) as results,
        tc.psum_pool(name="banks", bufs=BANKS) as banks,
    ):
        fields = held.tile([PIXELS, VOXELS], F32, name="fields")
        nc.sync.dma_start(fields[:], rf)
        offsets = held.tile([PIXELS, PICKED // 16], U16, name="offsets")
        nc.sync.dma_start(offsets[:], offs)
        maps = held.tile([PIXELS, IMAGES * CHANNELS], BF16, name="maps")
        nc.sync.dma_start(maps[:], fmap)
        weights = [held.tile([CHANNELS, PICKED // 2], F32, name=f"weights{h}") for h in range(2)]
        for h in range(2):
            nc.sync.dma_start(weights[h][:], w[:, h * PICKED // 2 : (h + 1) * PICKED // 2])

        scratch = held.tile([PIXELS, 1], F32, name="scratch")
        nc.vector.memset(scratch[:], 0.0)
        warmed = held.tile([PIXELS, 1], F32, name="warmed")
        nc.scalar.activation(warmed[:], scratch[:], COPY)

        starts = [sum(WIDTHS[:k]) for k in range(len(WIDTHS))]

        def look_up(k):
            start, width = starts[k], WIDTHS[k]
            picked = pieces.tile([PIXELS, width], F32, name="picked")
            listed = offsets[:, start // 16 : (start + width) // 16]
            nc.scalar.activation(picked[:], fields[:].indirect(listed), COPY)
            rectified = pieces.tile([PIXELS, width], BF16, name="rectified")
            if k < len(WIDTHS) - 1:
                nc.vector.scalar_tensor_tensor(rectified[:], picked[:], SLOPE, picked[:], MULT, MAX)
            else:
                lift = pieces.tile([PIXELS, width], F32, name="lift")
                nc.scalar.activation(lift[:], picked[:], RELU, scale=SLOPE - 1.0)
                nc.gpsimd.tensor_tensor(rectified[:], picked[:], lift[:], ADD)
            return rectified

        def pool_and_scale(k, rectified):
            width = WIDTHS[k]
            columns = slice(starts[k], starts[k] + width)
            sharings = [BLOCK // width] * (IMAGES * width // BLOCK)
            if k == 0:
                sharings = [1] * sharings[0] + sharings[1:]
            for n, sharing in enumerate(sharings):
                first = sum(sharings[:n])
                share = weights[starts[k] * 2 // PICKED]
                local = slice(starts[k] % (PICKED // 2), starts[k] % (PICKED // 2) + width)
                repeated = share[:, local].unsqueeze(1).to_broadcast([CHANNELS, sharing, width])
                pooled = banks.tile([CHANNELS, sharing, width], F32, name="pooled")
                for i in range(sharing):
                    rows = slice((first + i) * CHANNELS, (first + i + 1) * CHANNELS)
                    nc.tensor.matmul(pooled[:, i, :], maps[:, rows], rectified[:], start=True, stop=True)
                scaled = results.tile([CHANNELS, sharing, width], F32, name="scaled")
                nc.vector.tensor_tensor(scaled[:], pooled[:], repeated, MULT)
                block = out[first * CHANNELS : (first + sharing) * CHANNELS, columns]
                nc.sync.dma_start(block.rearrange("(i c) j -> c i j", c=CHANNELS), scaled[:])

        ready = look_up(0)
        for k in range(len(WIDTHS)):
            ahead = look_up(k + 1) if k + 1 < len(WIDTHS) else None
            pool_and_scale(k, ready)
            ready = ahead
